import numpy as np
import ml_dtypes


def mxq(x, axis, fmt="e4m3"):
    dtype, down = {"e4m3": (ml_dtypes.float8_e4m3fn, 7), "e5m2": (ml_dtypes.float8_e5m2, 14)}[fmt]
    v = np.moveaxis(np.asarray(x, np.float32).astype(ml_dtypes.bfloat16).astype(np.float64), axis, -1)
    blocks = v.reshape(v.shape[:-1] + (-1, 32))
    amax = np.abs(blocks).max(-1, keepdims=True)
    byte = np.maximum(np.where(amax > 0, np.frexp(amax)[1] - 1 + 127, 0) - down, 1)
    scale = np.exp2(byte - 127.0)
    codes = (blocks / scale).astype(np.float32).astype(dtype).astype(np.float64)
    return np.moveaxis((codes * scale).reshape(v.shape), -1, axis)


WIDE = False


def mx_kscale(k):
    if not WIDE:
        return np.ones(k)
    levels = np.array([10, -10, 5, -5, 0])
    if k % 512:
        return np.exp2(np.random.permutation(np.resize(levels, k // 32))).repeat(32)
    a = np.empty((k // 512, 16))
    for p in range(k // 512):
        a[p, :8] = np.random.permutation(np.resize(levels, 8))
        for g in range(8):
            far = levels[np.abs(levels - a[p, g]) >= 10]
            a[p, g + 8] = far[np.random.randint(len(far))]
    return np.exp2(a.ravel()).repeat(32)


BF16 = ml_dtypes.bfloat16


def bf(x):
    return np.asarray(x, np.float32).astype(BF16)


def f64(x):
    return np.asarray(x).astype(np.float64)


E2M1 = np.array([0.0, 0.5, 1.0, 1.5, 2.0, 3.0, 4.0, 6.0, -0.0, -0.5, -1.0, -1.5, -2.0, -3.0, -4.0, -6.0])


def pack_weight(w, fmt):
    k, n = w.shape
    w = f64(bf(w)).reshape(k // 32, 32, n)
    amax = np.abs(w).max(1)
    if fmt == "e4m3":
        byte = np.frexp(amax)[1] - 1 + 127 - 7
    else:
        mant, ex = np.frexp(amax / 6.0)
        byte = np.where(mant > 0.5, ex, ex - 1) + 127
    byte = np.clip(np.where(amax > 0, byte, 1), 1, 254)
    scaled = (w * np.exp2(127.0 - byte)[:, None, :]).reshape(k, n).astype(np.float32)
    by_word = np.ascontiguousarray(scaled.reshape(k // 512, 128, 4, n).transpose(0, 1, 3, 2))
    if fmt == "e4m3":
        words = by_word.astype(ml_dtypes.float8_e4m3fn).view(np.uint8)
    else:
        c = by_word.astype(ml_dtypes.float4_e2m1fn).view(np.uint8) & 0xF
        words = c[..., 0::2] | (c[..., 1::2] << 4)
    return np.ascontiguousarray(words), np.ascontiguousarray(byte.astype(np.uint8).reshape(k // 512, 16, n))


def unpack_weight(words, scales, fmt):
    g, p, n, _ = words.shape
    if fmt == "e4m3":
        vals = np.ascontiguousarray(words).view(ml_dtypes.float8_e4m3fn).astype(np.float64)
    else:
        nib = np.empty((g, p, n, 4), np.uint8)
        nib[..., 0::2] = words & 0xF
        nib[..., 1::2] = words >> 4
        vals = E2M1[nib]
    vals = vals * np.repeat(np.exp2(scales.astype(np.float64) - 127.0), 8, axis=1)[..., None]
    return vals.transpose(0, 1, 3, 2).reshape(g * 512, n)
def pack4(w):
    words, scales = pack_weight(w, "e2m1")
    return words.reshape(words.shape[0], 128, -1), scales


def unpack4(words, scales):
    return unpack_weight(words.reshape(words.shape[0], 128, -1, 2), scales, "e2m1")


B, N, DIN, DH, DOUT = 4096, 8, 64, 64, 64
KH = N * DH
KO = N * DOUT
EPS = 1e-5


def elu(v):
    return np.where(v > 0.0, v, np.expm1(np.minimum(v, 0.0)))


def sigmoid(v):
    return 1.0 / (1.0 + np.exp(-v))


def draw0():
    rn = np.random.standard_normal
    s, t = mx_kscale(KH), mx_kscale(KO)
    h = bf(elu(rn((B, KH))) * s)
    x = bf(rn((B, N, DIN)) + 0.5)
    cW1_words, cW1_scales = pack4(rn((KH, KO)) * 1.2 / np.sqrt(KH) / s[:, None] * t)
    cb1 = bf(rn(KO) * 0.3 * t)
    cW4_words, cW4_scales = pack4(rn((KO, KO)) / np.sqrt(KO) / t[:, None])
    cb4 = bf(rn(KO) * 0.3)
    cW5_words, cW5_scales = pack4(rn((KO, KO)) / np.sqrt(KO) / t[:, None])
    cb5 = bf(rn(KO) * 0.3)
    return {
        "h": h,
        "x": x,
        "cW1_words": cW1_words,
        "cW1_scales": cW1_scales,
        "cb1": cb1,
        "cW4_words": cW4_words,
        "cW4_scales": cW4_scales,
        "cb4": cb4,
        "cW5_words": cW5_words,
        "cW5_scales": cW5_scales,
        "cb5": cb5,
        "clng": bf(1.0 + 0.2 * rn(KO)),
        "clnb": bf(0.2 * rn(KO)),
    }


def core(h, x, cW1_words, cW1_scales, cb1, cW4_words, cW4_scales, cb4, cW5_words, cW5_scales, cb5, clng, clnb):
    flat = f64(x).reshape(B, N * DIN)
    e1 = (mxq(f64(h), 1, "e4m3") @ unpack4(cW1_words, cW1_scales)) + f64(cb1)
    e1q = mxq(e1, 1, "e4m3")
    g = sigmoid((e1q @ unpack4(cW4_words, cW4_scales)) + f64(cb4)) * ((e1q @ unpack4(cW5_words, cW5_scales)) + f64(cb5))
    r = flat + g
    c = (r - r.mean(-1, keepdims=True)) * (1.0 / np.sqrt(r.var(-1, keepdims=True) + EPS)) * f64(clng) + f64(clnb)
    c = c.reshape(B, N, DOUT)
    e = np.exp(c - c.max(1, keepdims=True))
    return e / e.sum(1, keepdims=True)


def e4m3fn_bytes(y):
    return np.clip(np.asarray(y, np.float64), -448.0, 448.0).astype(np.float32).astype(ml_dtypes.float8_e4m3fn).view(np.uint8)


def e4m3fn_values(b):
    return np.asarray(b, np.uint8).view(ml_dtypes.float8_e4m3fn).astype(np.float64)


def setup_inputs():
    d = draw0()
    x0 = np.asarray(d['h']).astype(np.float64)
    s = (np.max(np.abs(x0), axis=(0,), keepdims=True) / 448.0).astype(np.float32)
    out = {}
    for k, v in d.items():
        if k == 'h':
            out['h_bytes'] = e4m3fn_bytes(x0 / s.astype(np.float64))
            out['h_scale'] = s
        else:
            out[k] = v
    return out


def reference(h_bytes, h_scale, x, cW1_words, cW1_scales, cb1, cW4_words, cW4_scales, cb4, cW5_words, cW5_scales, cb5, clng, clnb):
    return core(e4m3fn_values(h_bytes) * h_scale.astype(np.float64), x, cW1_words, cW1_scales, cb1, cW4_words, cW4_scales, cb4, cW5_words, cW5_scales, cb5, clng, clnb)

from contextlib import ExitStack

import concourse.mybir as mybir
from concourse.masks import make_identity

F32 = mybir.dt.float32
BF16 = mybir.dt.bfloat16
U8 = mybir.dt.uint8
U32 = mybir.dt.uint32
I32 = mybir.dt.int32
F8 = mybir.dt.float8_e4m3fn
FP8X4 = mybir.dt.float8_e4m3fn_x4
FP4X4 = mybir.dt.float4_e2m1fn_x4
ALU = mybir.AluOpType
ACT = mybir.ActivationFunctionType
AX = mybir.AxisListType

P = 128
ROWS = 4096
K = 512
VARS = 8
FEAT = 64
Q = 4
GROUPS = ROWS // (P * Q)
TILES = ROWS // P
EPS = 1e-5
FLOPS = 3 * 2 * ROWS * K * K


def tile_variableselectionnetwork_pa_t_w4_kernel(
    tc, h_bytes, h_scale, x, cW1_words, cW1_scales, cb1, cW4_words, cW4_scales, cb4, cW5_words, cW5_scales, cb5, clng, clnb, out
):
    nc = tc.nc
    with ExitStack() as ctx:
        const = ctx.enter_context(tc.tile_pool(name="const", bufs=1))
        sb = ctx.enter_context(tc.tile_pool(name="sb", bufs=2))
        ps = ctx.enter_context(tc.psum_pool(name="ps", bufs=1))
        ctx.enter_context(tc.manual_schedule())

        h_view = h_bytes.rearrange("(g p q) k -> g p q k", p=P, q=Q)
        x_view = x.rearrange("(g p q) n d -> g p q (n d)", p=P, q=Q)
        out_view = out.rearrange("(g p q) n d -> g p q (n d)", p=P, q=Q)
        hb_in = []
        x_in = []
        for g in range(GROUPS):
            hb_in.append(const.tile([P, Q, K], U8, name="hbytes%d" % g))
            x_in.append(const.tile([P, Q, K], BF16, name="x%d" % g))
        hscale = const.tile([P, K], F32, name="hscale")
        w1raw = const.tile([P, 2 * K], U8, name="w1raw", align_bytes=64)
        w4 = const.tile([P, 2 * K], U8, name="w4", align_bytes=64)
        w5 = const.tile([P, 2 * K], U8, name="w5", align_bytes=64)
        w1sraw = const.tile([P, K], U8, name="w1sraw", align_bytes=64)
        w4s = const.tile([P, K], U8, name="w4s", align_bytes=64)
        w5s = const.tile([P, K], U8, name="w5s", align_bytes=64)
        cb1t = const.tile([P, 4], BF16, name="cb1t")
        vecs = const.tile([P, P], BF16, name="vecs")

        for sp in (w1sraw, w4s, w5s):
            nc.vector.memset(sp[:].bitcast(I32), 0)
        nc.vector.memset(vecs[:], 0.0)

        def load_scales(dst, src):
            for quad in range(4):
                nc.sync.dma_start(
                    out=dst[32 * quad : 32 * quad + 4, :].bitcast(I32), in_=src[0, 4 * quad : 4 * quad + 4, :].bitcast(I32)
                )

        nc.sync.dma_start(out=hb_in[0][:], in_=h_view[0])
        nc.sync.dma_start(out=hscale[:], in_=h_scale.rearrange("o k -> (o k)").partition_broadcast(P))
        nc.sync.dma_start(out=w1raw[:], in_=cW1_words[0])
        load_scales(w1sraw, cW1_scales)
        nc.sync.dma_start(out=cb1t[:], in_=cb1.rearrange("(p t) -> p t", t=4))
        for j, vec in enumerate((cb4, cb5, clng, clnb)):
            nc.sync.dma_start(out=vecs[4 * j : 4 * j + 4, :], in_=vec.rearrange("(t p) -> t p", p=P))
        nc.sync.dma_start(out=w4[:], in_=cW4_words[0])
        nc.sync.dma_start(out=w5[:], in_=cW5_words[0])
        load_scales(w4s, cW4_scales)
        load_scales(w5s, cW5_scales)
        nc.sync.dma_start(out=x_in[0][:], in_=x_view[0])
        for g in range(1, GROUPS):
            nc.sync.dma_start(out=hb_in[g][:], in_=h_view[g])
            nc.sync.dma_start(out=x_in[g][:], in_=x_view[g])

        idf = const.tile([P, P], F32, name="idf")
        make_identity(nc, idf[:])
        idb = const.tile([P, P], BF16, name="idb")
        nc.vector.tensor_copy(out=idb[:], in_=idf[:])
        id2 = const.tile([P, P], BF16, name="id2")
        nc.vector.tensor_scalar(out=id2[:], in0=idf[:], scalar1=2.0, scalar2=None, op0=ALU.mult)
        swp = const.tile([P, P], F32, name="swp")
        nc.vector.tensor_copy(out=swp[:, 0:64], in_=idf[:, 64:128])
        nc.vector.tensor_copy(out=swp[:, 64:128], in_=idf[:, 0:64])
        mhalf = const.tile([P, 1], F32, name="mhalf")
        nc.vector.memset(mhalf[:], -0.5)
        warm = const.tile([P, 1], F32, name="warm")
        nc.scalar.activation(out=warm[:], in_=mhalf[:], func=ACT.Exp)

        w1 = const.tile([P, 4, 2 * P], U8, name="w1", align_bytes=64)
        w1s = const.tile([P, 4, P], U8, name="w1s", align_bytes=64)
        nc.vector.tensor_copy(
            out=w1[:].rearrange("p t (m b) -> p t m b", b=2), in_=w1raw[:].rearrange("p (m t b) -> p t m b", t=4, b=2)
        )
        nc.vector.tensor_copy(out=w1s[:], in_=w1sraw[:].rearrange("p (m t) -> p t m", t=4))

        ptv = ps.tile([P, P], BF16, name="ptv", tag="tr", bufs=1)
        nc.tensor.transpose(ptv[:], vecs[:], idb[:])
        cols = const.tile([P, 16], F32, name="cols")
        nc.vector.tensor_copy(out=cols[:], in_=ptv[:, 0:16])
        hcb4 = const.tile([P, 4], F32, name="hcb4")
        nc.vector.tensor_scalar(out=hcb4[:], in0=cols[:, 0:4], scalar1=0.5, scalar2=None, op0=ALU.mult)

        hb, hs, pht, hg, hq, hqs, p1, e1 = {}, {}, {}, {}, {}, {}, {}, {}
        eq, eqs = {}, {}
        p4, p5, th, t1, gt = {}, {}, {}, {}, {}
        pr, mv, rs, nm, nn, pn, ct = {}, {}, {}, {}, {}, {}, {}
        pc, mx, dd, ee, pss, sts, sall, inv, oo = {}, {}, {}, {}, {}, {}, {}, {}, {}

        def cast(i):
            hb[i] = sb.tile([P, K], BF16, name="hb", tag="hb", bufs=3)
            nc.scalar.copy(out=hb[i][:], in_=hb_in[i // Q][:, i % Q, :].bitcast(F8))

        def prod(i):
            hs[i] = sb.tile([P, K], BF16, name="hs", tag="hs", bufs=3)
            nc.gpsimd.tensor_tensor(out=hs[i][:], in0=hb[i][:], in1=hscale[:], op=ALU.mult)

        def htr(i):
            pht[i] = ps.tile([P, 2, P], F32, name="pht", tag="tr", bufs=1)
            words = hs[i][:].bitcast(F32)
            for u in range(2):
                nc.tensor.transpose(pht[i][:, u, :], words[:, u : 2 * P : 2], idf[:])

        def hev(i):
            hg[i] = sb.tile([P, P, 4], BF16, name="hg", tag="hg", bufs=3, align_bytes=64)
            nc.scalar.copy(
                out=hg[i][:].rearrange("p r t -> p (r t)").bitcast(F32).rearrange("p (r u) -> p r u", u=2),
                in_=pht[i][:].rearrange("p u r -> p r u"),
            )

        def hquant(i):
            hq[i] = sb.tile([P, P], U32, name="hq", tag="hq", bufs=3, align_bytes=64)
            hqs[i] = sb.tile([P, P], U8, name="hqs", tag="hqs", bufs=3, align_bytes=64)
            nc.vector.quantize_mx(out=hq[i][:].bitcast(FP8X4), scales=hqs[i][:], in_=hg[i][:].rearrange("p r t -> p (r t)"))

        def s1(i):
            p1[i] = ps.tile([P, 4, P], F32, name="p1", tag="p1", bufs=1)
            for t in range(4):
                nc.tensor.matmul_mx(
                    out=p1[i][:, t, :],
                    lhsT=w1[:, t, :].bitcast(FP4X4),
                    lhsT_scale=w1s[:, t, :],
                    rhs=hq[i][:].bitcast(FP8X4),
                    rhs_scale=hqs[i][:],
                    start=True,
                    stop=True,
                )

        def e1add(i):
            e1[i] = sb.tile([P, P, 4], BF16, name="e1", tag="e1", bufs=3, align_bytes=64)
            nc.vector.tensor_tensor(
                out=e1[i][:],
                in0=p1[i][:].rearrange("p t r -> p r t"),
                in1=cb1t[:].unsqueeze(1).to_broadcast([P, P, 4]),
                op=ALU.add,
            )

        def equant(i):
            g, q = i // Q, i % Q
            if q == 0:
                eq[g] = sb.tile([P, Q * P], U32, name="eq", tag="eq", bufs=3, align_bytes=64)
                eqs[g] = sb.tile([P, Q * P], U8, name="eqs", tag="eqs", bufs=3, align_bytes=64)
            cs = slice(q * P, (q + 1) * P)
            nc.vector.quantize_mx(
                out=eq[g][:, cs].bitcast(FP8X4), scales=eqs[g][:, cs], in_=e1[i][:].rearrange("p r t -> p (r t)")
            )

        def s2(g, t):
            p4[g, t] = ps.tile([P, Q * P], F32, name="p4", tag="p4", bufs=1)
            p5[g, t] = ps.tile([P, Q * P], F32, name="p5", tag="p5", bufs=1)
            for pt, w, ws in ((p4[g, t], w4, w4s), (p5[g, t], w5, w5s)):
                nc.tensor.matmul_mx(
                    out=pt[:],
                    lhsT=w[:, 2 * P * t : 2 * P * (t + 1)].bitcast(FP4X4),
                    lhsT_scale=ws[:, P * t : P * (t + 1)],
                    rhs=eq[g][:].bitcast(FP8X4),
                    rhs_scale=eqs[g][:],
                    start=True,
                    stop=True,
                )

        def tanh(g, t):
            th[g, t] = sb.tile([P, Q * P], F32, name="th", tag="th", bufs=2)
            nc.scalar.activation(out=th[g, t][:], in_=p4[g, t][:], func=ACT.Tanh, bias=hcb4[:, t : t + 1], scale=0.5)

        def plus1(g, t):
            t1[g, t] = sb.tile([P, Q * P], F32, name="t1", tag="t1", bufs=2)
            nc.gpsimd.tensor_scalar(out=t1[g, t][:], in0=th[g, t][:], scalar1=1.0, scalar2=1.0, op0=ALU.mult, op1=ALU.add)

        def gate(g, t):
            if t == 0:
                gt[g] = sb.tile([P, 4, Q * P], F32, name="gt", tag="gt", bufs=2)
            nc.vector.scalar_tensor_tensor(
                out=gt[g][:, t, :], in0=p5[g, t][:], scalar=cols[:, 4 + t : 5 + t], in1=t1[g, t][:], op0=ALU.add, op1=ALU.mult
            )

        def rsum(i):
            g, q = i // Q, i % Q
            pr[i] = ps.tile([P, K], F32, name="pr", tag="pr", bufs=2)
            nc.tensor.matmul(out=pr[i][:], lhsT=id2[:], rhs=x_in[g][:, q, :], start=True, stop=False)
            for t in range(4):
                nc.tensor.matmul(
                    out=pr[i][:, t * P : (t + 1) * P],
                    lhsT=gt[g][:, t, q * P : (q + 1) * P],
                    rhs=idf[:],
                    start=False,
                    stop=(t == 3),
                    is_transpose=True,
                )

        st = {}

        def bn(i):
            st[i] = sb.tile([P, 6], F32, name="st", tag="st", bufs=3)
            nc.vector.bn_stats(out=st[i][:], in_=pr[i][:])

        def aggr(i):
            mv[i] = sb.tile([P, 2], F32, name="mv", tag="mv", bufs=3)
            nc.vector.bn_aggr(out=mv[i][:], in_=st[i][:])

        def rstd(i):
            rs[i] = sb.tile([P, 1], F32, name="rs", tag="rs", bufs=3)
            nm[i] = sb.tile([P, 1], F32, name="nm", tag="nm", bufs=3)
            ve = sb.tile([P, 1], F32, name="ve", tag="ve", bufs=3)
            nc.gpsimd.tensor_scalar(out=ve[:], in0=mv[i][:, 1:2], scalar1=4.0 * EPS, scalar2=None, op0=ALU.add)
            nc.gpsimd.tensor_tensor(out=rs[i][:], in0=ve[:], in1=mhalf[:], op=ALU.pow)
            nc.gpsimd.tensor_scalar(
                out=nm[i][:], in0=mv[i][:, 0:1], scalar1=rs[i][:], scalar2=-1.0, op0=ALU.mult, op1=ALU.mult
            )

        def norm(i):
            nn[i] = sb.tile([P, K], F32, name="nn", tag="nn", bufs=12)
            nc.scalar.activation(out=nn[i][:], in_=pr[i][:], func=ACT.Identity, bias=nm[i][:], scale=rs[i][:])

        def ntr(g, t):
            pn[g, t] = ps.tile([P, Q * P], F32, name="pn", tag="tr", bufs=1)
            for q in range(Q):
                nc.tensor.transpose(pn[g, t][:, q * P : (q + 1) * P], nn[g * Q + q][:, t * P : (t + 1) * P], idf[:])

        def affine(g, t):
            if t == 0:
                ct[g] = sb.tile([P, 4, Q * P], F32, name="ct", tag="ct", bufs=2)
            nc.scalar.activation(
                out=ct[g][:, t, :], in_=pn[g, t][:], func=ACT.Identity, bias=cols[:, 12 + t : 13 + t], scale=cols[:, 8 + t : 9 + t]
            )

        def ctr(i):
            g, q = i // Q, i % Q
            pc[i] = ps.tile([P, K], F32, name="pc", tag="pc", bufs=1)
            for t in range(4):
                nc.tensor.transpose(pc[i][:, t * P : (t + 1) * P], ct[g][:, t, q * P : (q + 1) * P], idf[:])

        def cmax(i):
            mx[i] = sb.tile([P, FEAT], F32, name="mx", tag="mx", bufs=3)
            nc.vector.tensor_reduce(out=mx[i][:], in_=pc[i][:].rearrange("p (n j) -> p j n", j=FEAT), axis=AX.X, op=ALU.max)

        def csub(i):
            dd[i] = sb.tile([P, VARS, FEAT], F32, name="dd", tag="dd", bufs=3)
            nc.vector.tensor_tensor(
                out=dd[i][:],
                in0=pc[i][:].rearrange("p (n j) -> p n j", j=FEAT),
                in1=mx[i][:].unsqueeze(1).to_broadcast([P, VARS, FEAT]),
                op=ALU.subtract,
            )

        def cexp(i):
            ee[i] = sb.tile([P, VARS, FEAT], F32, name="ee", tag="ee", bufs=14)
            nc.scalar.activation(out=ee[i][:], in_=dd[i][:], func=ACT.Exp)

        def strn(i):
            pss[i] = ps.tile([P, 2, P], F32, name="pss", tag="pss", bufs=1)
            flat = ee[i][:].rearrange("p n j -> p (n j)")
            for a in range(4):
                nc.tensor.matmul(
                    out=pss[i][:, 0, :], lhsT=flat[:, a * P : (a + 1) * P], rhs=idf[:], start=(a == 0), stop=(a == 3), is_transpose=True
                )

        def sev(i):
            sts[i] = sb.tile([P, P], F32, name="sts", tag="sts", bufs=2)
            nc.scalar.copy(out=sts[i][:], in_=pss[i][:, 0, :])

        def sback(i):
            for a, m in enumerate((idf, swp)):
                nc.tensor.matmul(out=pss[i][:, 1, :], lhsT=sts[i][:], rhs=m[:], start=(a == 0), stop=(a == 1), is_transpose=True)

        def scopy(i):
            g, q = i // Q, i % Q
            if q == 0:
                sall[g] = sb.tile([P, Q, FEAT], F32, name="sall", tag="sall", bufs=2)
            nc.vector.tensor_copy(out=sall[g][:, q, :], in_=pss[i][:, 1, 0:FEAT])

        pp2, pp4, rr4, rr2 = {}, {}, {}, {}

        def recip_a(g):
            s = sall[g]
            pp2[g] = sb.tile([P, 2, FEAT], F32, name="pp2", tag="pp2", bufs=2)
            nc.vector.tensor_tensor(out=pp2[g][:], in0=s[:, 0:2, :], in1=s[:, 2:4, :], op=ALU.mult)

        def recip_b(g):
            pp4[g] = sb.tile([P, FEAT], F32, name="pp4", tag="pp4", bufs=2)
            nc.vector.tensor_tensor(out=pp4[g][:], in0=pp2[g][:, 0, :], in1=pp2[g][:, 1, :], op=ALU.mult)

        def recip_c(g):
            rr4[g] = sb.tile([P, FEAT], F32, name="rr4", tag="rr4", bufs=2)
            nc.vector.reciprocal(out=rr4[g][:], in_=pp4[g][:])

        def recip_d(g):
            rr2[g] = sb.tile([P, 2, FEAT], F32, name="rr2", tag="rr2", bufs=2)
            for a in range(2):
                nc.vector.tensor_tensor(out=rr2[g][:, a, :], in0=rr4[g][:], in1=pp2[g][:, 1 - a, :], op=ALU.mult)

        def recip_e(g):
            s = sall[g]
            inv[g] = sb.tile([P, Q, FEAT], F32, name="inv", tag="inv", bufs=2)
            nc.vector.tensor_tensor(out=inv[g][:, 0:2, :], in0=rr2[g][:], in1=s[:, 2:4, :], op=ALU.mult)
            nc.vector.tensor_tensor(out=inv[g][:, 2:4, :], in0=rr2[g][:], in1=s[:, 0:2, :], op=ALU.mult)

        def mult(i):
            g, q = i // Q, i % Q
            oo[i] = sb.tile([P, VARS, FEAT], F32, name="oo", tag="oo", bufs=4)
            nc.gpsimd.tensor_tensor(
                out=oo[i][:], in0=ee[i][:], in1=inv[g][:, q, :].unsqueeze(1).to_broadcast([P, VARS, FEAT]), op=ALU.mult
            )

        def store(i):
            g, q = i // Q, i % Q
            nc.sync.dma_start(out=out_view[g][:, q, :], in_=oo[i][:].rearrange("p n j -> p (n j)"))

        def on(fn, i):
            if 0 <= i < TILES:
                fn(i)

        def ong(fn, s):
            if 0 <= s < TILES:
                fn(s // Q, s % Q)

        def once(fn, s):
            if 0 <= s < TILES and s % Q == 0:
                fn(s // Q)

        for k in range(1, TILES + 35):
            on(norm, k - 17)
            ong(plus1, k - 11)
            on(sev, k - 26)
            on(e1add, k - 6)
            on(htr, k - 4)
            on(hev, k - 4)
            on(ctr, k - 24)
            on(rstd, k - 16)
            on(rsum, k - 15)
            ong(ntr, k - 20)
            on(cast, k - 1)
            on(cmax, k - 24)
            on(sback, k - 26)
            ong(gate, k - 11)
            on(cexp, k - 25)
            on(scopy, k - 26)
            on(mult, k - 34)
            on(csub, k - 24)
            on(bn, k - 15)
            on(prod, k - 3)
            once(recip_e, k - 33)
            once(recip_d, k - 32)
            once(recip_a, k - 29)
            ong(s2, k - 10)
            on(hquant, k - 4)
            on(store, k - 35)
            on(equant, k - 6)
            ong(affine, k - 20)
            once(recip_b, k - 30)
            on(s1, k - 5)
            ong(tanh, k - 10)
            on(strn, k - 25)
            once(recip_c, k - 31)
            on(aggr, k - 15)
